import numpy as np
import ml_dtypes

BF16 = ml_dtypes.bfloat16


def bf(x):
    return np.asarray(x, np.float32).astype(BF16)


def f32(x):
    return np.asarray(x, np.float32)


def f64(x):
    return np.asarray(x).astype(np.float64)


def striped(idx):
    return np.tile(idx.reshape(-1, 16).T, (8, 1))


T, D, S, N = 256, 128, 256, 128
TEMPERATURE = 0.1


def setup_inputs():
    return {
        "x": bf(np.random.standard_normal((D, T)) * np.sqrt(2.0 / D)),
        "centroids": bf(np.random.standard_normal((D, N)) * np.sqrt(2.0 / (N + D))),
        "base": f32(0.1 * np.abs(np.random.standard_normal((T, S)))),
        "offs": striped(np.random.permutation(S)[:N]),
    }


def reference(x, centroids, base, offs):
    idx = offs[:16].T.reshape(-1)
    xs = f64(x)
    cs = f64(centroids)
    cross = xs.T @ cs
    c_sq = np.sum(cs * cs, axis=0)
    l = (2.0 * cross - c_sq[None, :]) / TEMPERATURE
    e = np.exp(l - np.max(l, axis=1, keepdims=True))
    r = 1.0 / np.sum(e, axis=1, keepdims=True)
    out = f64(base).copy()
    out[:, idx] = e * r
    return out

@@ -1,0 +1,63 @@
+import concourse.mybir as mybir
+
+F32 = mybir.dt.float32
+BF16 = mybir.dt.bfloat16
+U16 = mybir.dt.uint16
+MULT = mybir.AluOpType.mult
+EXP = mybir.ActivationFunctionType.Exp
+AXIS_X = mybir.AxisListType.X
+
+P = 128
+T, D, S, N = 256, 128, 256, 128
+TEMPERATURE = 0.1
+LOGIT_SCALE = 2.0 / TEMPERATURE
+
+FLOPS = 2 * T * D * N + 2 * D * N
+
+
+def tile_differentiablekmeanslayer_kernel(tc, x, centroids, base, offs, out):
+    nc = tc.nc
+    with (
+        tc.tile_pool(name="held", bufs=1) as held,
+        tc.tile_pool(name="work", bufs=2) as work,
+        tc.psum_pool(name="psum", bufs=2) as psum,
+    ):
+        x_sb = held.tile([D, T], BF16, name="x_sb")
+        nc.sync.dma_start(x_sb[:], x)
+        c_sb = held.tile([D, N], BF16, name="c_sb")
+        nc.scalar.dma_start(c_sb[:], centroids)
+        offsets = held.tile([P, N // 16], U16, name="offsets")
+        nc.sync.dma_start(offsets[:], offs)
+
+        minus_half = held.tile([D, P], BF16, name="minus_half")
+        nc.vector.memset(minus_half[:], -0.5)
+        ones = held.tile([P, N], F32, name="ones")
+        nc.vector.memset(ones[:], 1.0)
+        c_squares = held.tile([D, N], BF16, name="c_squares")
+        nc.vector.tensor_tensor(c_squares[:], c_sb[:], c_sb[:], MULT)
+
+        for block in range(T // P):
+            tokens = slice(block * P, (block + 1) * P)
+
+            window = work.tile([P, S], F32, name="window")
+            nc.sync.dma_start(window[:], base[tokens, :])
+
+            half_logits = psum.tile([P, N], F32, name="half_logits")
+            nc.tensor.matmul(half_logits[:], x_sb[:, tokens], c_sb[:], start=True, stop=False)
+            nc.tensor.matmul(half_logits[:], minus_half[:], c_squares[:], start=False, stop=True)
+
+            row_max = work.tile([P, 1], F32, name="row_max")
+            nc.vector.reduce_max(row_max[:], half_logits[:], axis=AXIS_X)
+            minus_m = work.tile([P, 1], F32, name="minus_m")
+            nc.vector.tensor_scalar(minus_m[:], row_max[:], -LOGIT_SCALE, None, MULT)
+            e = work.tile([P, N], F32, name="e")
+            e_sum = work.tile([P, 1], F32, name="e_sum")
+            nc.scalar.activation(e[:], half_logits[:], EXP, bias=minus_m[:], scale=LOGIT_SCALE, accum_out=e_sum[:])
+            r = work.tile([P, 1], F32, name="r")
+            nc.vector.reciprocal(r[:], e_sum[:])
+
+            r_row = work.tile([P, N], F32, name="r_row")
+            nc.vector.tensor_scalar(r_row[:], ones[:], r[:], None, MULT)
+
+            nc.vector.tensor_tensor(window[:].indirect(offsets[:]), e[:], r_row[:], MULT)
+            nc.sync.dma_start(out[tokens, :], window[:])

@@ -4,8 +4,8 @@ F32 = mybir.dt.float32
 BF16 = mybir.dt.bfloat16
 U16 = mybir.dt.uint16
 MULT = mybir.AluOpType.mult
+MIN = mybir.AluOpType.min
 EXP = mybir.ActivationFunctionType.Exp
-AXIS_X = mybir.AxisListType.X
 
 P = 128
 T, D, S, N = 256, 128, 256, 128
@@ -46,13 +46,12 @@ def tile_differentiablekmeanslayer_kernel(tc, x, centroids, base, offs, out):
             nc.tensor.matmul(half_logits[:], x_sb[:, tokens], c_sb[:], start=True, stop=False)
             nc.tensor.matmul(half_logits[:], minus_half[:], c_squares[:], start=False, stop=True)
 
-            row_max = work.tile([P, 1], F32, name="row_max")
-            nc.vector.reduce_max(row_max[:], half_logits[:], axis=AXIS_X)
+            minus_l = work.tile([P, N], F32, name="minus_l")
             minus_m = work.tile([P, 1], F32, name="minus_m")
-            nc.vector.tensor_scalar(minus_m[:], row_max[:], -LOGIT_SCALE, None, MULT)
+            nc.vector.tensor_scalar(minus_l[:], half_logits[:], -LOGIT_SCALE, None, MULT, MIN, accum_out=minus_m[:])
             e = work.tile([P, N], F32, name="e")
             e_sum = work.tile([P, 1], F32, name="e_sum")
-            nc.scalar.activation(e[:], half_logits[:], EXP, bias=minus_m[:], scale=LOGIT_SCALE, accum_out=e_sum[:])
+            nc.scalar.activation(e[:], minus_l[:], EXP, bias=minus_m[:], scale=-1.0, accum_out=e_sum[:])
             r = work.tile([P, 1], F32, name="r")
             nc.vector.reciprocal(r[:], e_sum[:])
 

@@ -6,6 +6,7 @@ U16 = mybir.dt.uint16
 MULT = mybir.AluOpType.mult
 MIN = mybir.AluOpType.min
 EXP = mybir.ActivationFunctionType.Exp
+COPY = mybir.ActivationFunctionType.Copy
 
 P = 128
 T, D, S, N = 256, 128, 256, 128
@@ -36,11 +37,15 @@ def tile_differentiablekmeanslayer_kernel(tc, x, centroids, base, offs, out):
         c_squares = held.tile([D, N], BF16, name="c_squares")
         nc.vector.tensor_tensor(c_squares[:], c_sb[:], c_sb[:], MULT)
 
-        for block in range(T // P):
+        blocks = range(T // P)
+        windows, es, e_sums, r_rows = [], [], [], []
+
+        for block in blocks:
             tokens = slice(block * P, (block + 1) * P)
 
             window = work.tile([P, S], F32, name="window")
             nc.sync.dma_start(window[:], base[tokens, :])
+            windows.append(window)
 
             half_logits = psum.tile([P, N], F32, name="half_logits")
             nc.tensor.matmul(half_logits[:], x_sb[:, tokens], c_sb[:], start=True, stop=False)
@@ -52,11 +57,20 @@ def tile_differentiablekmeanslayer_kernel(tc, x, centroids, base, offs, out):
             e = work.tile([P, N], F32, name="e")
             e_sum = work.tile([P, 1], F32, name="e_sum")
             nc.scalar.activation(e[:], minus_l[:], EXP, bias=minus_m[:], scale=-1.0, accum_out=e_sum[:])
+            es.append(e)
+            e_sums.append(e_sum)
+
+        for block in blocks:
             r = work.tile([P, 1], F32, name="r")
-            nc.vector.reciprocal(r[:], e_sum[:])
-
+            nc.vector.reciprocal(r[:], e_sums[block][:])
             r_row = work.tile([P, N], F32, name="r_row")
-            nc.vector.tensor_scalar(r_row[:], ones[:], r[:], None, MULT)
+            if block == 0:
+                nc.vector.tensor_scalar(r_row[:], ones[:], r[:], None, MULT)
+            else:
+                nc.scalar.activation(r_row[:], ones[:], COPY, scale=r[:])
+            r_rows.append(r_row)
 
-            nc.vector.tensor_tensor(window[:].indirect(offsets[:]), e[:], r_row[:], MULT)
-            nc.sync.dma_start(out[tokens, :], window[:])
+        for block in blocks:
+            tokens = slice(block * P, (block + 1) * P)
+            nc.vector.tensor_tensor(windows[block][:].indirect(offsets[:]), es[block][:], r_rows[block][:], MULT)
+            nc.sync.dma_start(out[tokens, :], windows[block][:])

@@ -23,10 +23,10 @@ def tile_differentiablekmeanslayer_kernel(tc, x, centroids, base, offs, out):
         tc.tile_pool(name="work", bufs=2) as work,
         tc.psum_pool(name="psum", bufs=2) as psum,
     ):
-        x_sb = held.tile([D, T], BF16, name="x_sb")
-        nc.sync.dma_start(x_sb[:], x)
         c_sb = held.tile([D, N], BF16, name="c_sb")
-        nc.scalar.dma_start(c_sb[:], centroids)
+        nc.sync.dma_start(c_sb[:], centroids)
+        x_sb = held.tile([D, T], BF16, name="x_sb")
+        nc.scalar.dma_start(x_sb[:], x)
         offsets = held.tile([P, N // 16], U16, name="offsets")
         nc.sync.dma_start(offsets[:], offs)
 

@@ -65,7 +65,7 @@ def tile_differentiablekmeanslayer_kernel(tc, x, centroids, base, offs, out):
             nc.vector.reciprocal(r[:], e_sums[block][:])
             r_row = work.tile([P, N], F32, name="r_row")
             if block == 0:
-                nc.vector.tensor_scalar(r_row[:], ones[:], r[:], None, MULT)
+                nc.vector.tensor_copy(r_row[:], r[:].to_broadcast([P, N]))
             else:
                 nc.scalar.activation(r_row[:], ones[:], COPY, scale=r[:])
             r_rows.append(r_row)

@@ -48,8 +48,12 @@ def tile_differentiablekmeanslayer_kernel(tc, x, centroids, base, offs, out):
             windows.append(window)
 
             half_logits = psum.tile([P, N], F32, name="half_logits")
-            nc.tensor.matmul(half_logits[:], x_sb[:, tokens], c_sb[:], start=True, stop=False)
-            nc.tensor.matmul(half_logits[:], minus_half[:], c_squares[:], start=False, stop=True)
+            if block == 0:
+                nc.tensor.matmul(half_logits[:], x_sb[:, tokens], c_sb[:], start=True, stop=False)
+                nc.tensor.matmul(half_logits[:], minus_half[:], c_squares[:], start=False, stop=True)
+            else:
+                nc.tensor.matmul(half_logits[:], minus_half[:], c_squares[:], start=True, stop=False)
+                nc.tensor.matmul(half_logits[:], x_sb[:, tokens], c_sb[:], start=False, stop=True)
 
             minus_l = work.tile([P, N], F32, name="minus_l")
             minus_m = work.tile([P, 1], F32, name="minus_m")

@@ -40,11 +40,14 @@ def tile_differentiablekmeanslayer_kernel(tc, x, centroids, base, offs, out):
         blocks = range(T // P)
         windows, es, e_sums, r_rows = [], [], [], []
 
+        base_blocks = base.rearrange("(p b) s -> b p s", b=T // P)
+        out_blocks = out.rearrange("(p b) s -> b p s", b=T // P)
+
         for block in blocks:
-            tokens = slice(block * P, (block + 1) * P)
+            tokens = slice(block, T, T // P)
 
             window = work.tile([P, S], F32, name="window")
-            nc.sync.dma_start(window[:], base[tokens, :])
+            nc.sync.dma_start(window[:], base_blocks[block])
             windows.append(window)
 
             half_logits = psum.tile([P, N], F32, name="half_logits")
@@ -75,6 +78,5 @@ def tile_differentiablekmeanslayer_kernel(tc, x, centroids, base, offs, out):
             r_rows.append(r_row)
 
         for block in blocks:
-            tokens = slice(block * P, (block + 1) * P)
             nc.vector.tensor_tensor(windows[block][:].indirect(offsets[:]), es[block][:], r_rows[block][:], MULT)
-            nc.sync.dma_start(out[tokens, :], windows[block][:])
+            nc.sync.dma_start(out_blocks[block], windows[block][:])

@@ -72,7 +72,7 @@ def tile_differentiablekmeanslayer_kernel(tc, x, centroids, base, offs, out):
             nc.vector.reciprocal(r[:], e_sums[block][:])
             r_row = work.tile([P, N], F32, name="r_row")
             if block == 0:
-                nc.vector.tensor_copy(r_row[:], r[:].to_broadcast([P, N]))
+                nc.vector.tensor_scalar(r_row[:], ones[:], r[:], None, MULT)
             else:
                 nc.scalar.activation(r_row[:], ones[:], COPY, scale=r[:])
             r_rows.append(r_row)

import concourse.mybir as mybir

F32 = mybir.dt.float32
BF16 = mybir.dt.bfloat16
U16 = mybir.dt.uint16
MULT = mybir.AluOpType.mult
MIN = mybir.AluOpType.min
EXP = mybir.ActivationFunctionType.Exp
COPY = mybir.ActivationFunctionType.Copy

P = 128
T, D, S, N = 256, 128, 256, 128
TEMPERATURE = 0.1
LOGIT_SCALE = 2.0 / TEMPERATURE

FLOPS = 2 * T * D * N + 2 * D * N


def tile_differentiablekmeanslayer_kernel(tc, x, centroids, base, offs, out):
    nc = tc.nc
    with (
        tc.tile_pool(name="held", bufs=1) as held,
        tc.tile_pool(name="work", bufs=2) as work,
        tc.psum_pool(name="psum", bufs=2) as psum,
    ):
        c_sb = held.tile([D, N], BF16, name="c_sb")
        nc.sync.dma_start(c_sb[:], centroids)
        x_sb = held.tile([D, T], BF16, name="x_sb")
        nc.scalar.dma_start(x_sb[:], x)
        offsets = held.tile([P, N // 16], U16, name="offsets")
        nc.sync.dma_start(offsets[:], offs)

        minus_half = held.tile([D, P], BF16, name="minus_half")
        nc.vector.memset(minus_half[:], -0.5)
        ones = held.tile([P, N], F32, name="ones")
        nc.vector.memset(ones[:], 1.0)
        c_squares = held.tile([D, N], BF16, name="c_squares")
        nc.vector.tensor_tensor(c_squares[:], c_sb[:], c_sb[:], MULT)

        blocks = range(T // P)
        windows, es, e_sums, r_rows = [], [], [], []

        base_blocks = base.rearrange("(p b) s -> b p s", b=T // P)
        out_blocks = out.rearrange("(p b) s -> b p s", b=T // P)

        for block in blocks:
            tokens = slice(block, T, T // P)

            window = work.tile([P, S], F32, name="window")
            nc.sync.dma_start(window[:], base_blocks[block])
            windows.append(window)

            half_logits = psum.tile([P, N], F32, name="half_logits")
            if block == 0:
                nc.tensor.matmul(half_logits[:], x_sb[:, tokens], c_sb[:], start=True, stop=False)
                nc.tensor.matmul(half_logits[:], minus_half[:], c_squares[:], start=False, stop=True)
            else:
                nc.tensor.matmul(half_logits[:], minus_half[:], c_squares[:], start=True, stop=False)
                nc.tensor.matmul(half_logits[:], x_sb[:, tokens], c_sb[:], start=False, stop=True)

            minus_l = work.tile([P, N], F32, name="minus_l")
            minus_m = work.tile([P, 1], F32, name="minus_m")
            nc.vector.tensor_scalar(minus_l[:], half_logits[:], -LOGIT_SCALE, None, MULT, MIN, accum_out=minus_m[:])
            e = work.tile([P, N], F32, name="e")
            e_sum = work.tile([P, 1], F32, name="e_sum")
            nc.scalar.activation(e[:], minus_l[:], EXP, bias=minus_m[:], scale=-1.0, accum_out=e_sum[:])
            es.append(e)
            e_sums.append(e_sum)

        for block in blocks:
            r = work.tile([P, 1], F32, name="r")
            nc.vector.reciprocal(r[:], e_sums[block][:])
            r_row = work.tile([P, N], F32, name="r_row")
            if block == 0:
                nc.vector.tensor_scalar(r_row[:], ones[:], r[:], None, MULT)
            else:
                nc.scalar.activation(r_row[:], ones[:], COPY, scale=r[:])
            r_rows.append(r_row)

        for block in blocks:
            nc.vector.tensor_tensor(windows[block][:].indirect(offsets[:]), es[block][:], r_rows[block][:], MULT)
            nc.sync.dma_start(out_blocks[block], windows[block][:])
